import numpy as np
import ml_dtypes


def mxq(x, axis, fmt="e4m3"):
    dtype, down = {"e4m3": (ml_dtypes.float8_e4m3fn, 7), "e5m2": (ml_dtypes.float8_e5m2, 14)}[fmt]
    v = np.moveaxis(np.asarray(x, np.float32).astype(ml_dtypes.bfloat16).astype(np.float64), axis, -1)
    blocks = v.reshape(v.shape[:-1] + (-1, 32))
    amax = np.abs(blocks).max(-1, keepdims=True)
    byte = np.maximum(np.where(amax > 0, np.frexp(amax)[1] - 1 + 127, 0) - down, 1)
    scale = np.exp2(byte - 127.0)
    codes = (blocks / scale).astype(np.float32).astype(dtype).astype(np.float64)
    return np.moveaxis((codes * scale).reshape(v.shape), -1, axis)


WIDE = False


def mx_kscale(k):
    if not WIDE:
        return np.ones(k)
    levels = np.array([10, -10, 5, -5, 0])
    a = np.random.permutation(np.resize(levels, k // 512 * 4)).reshape(k // 512, 4)
    idx = np.arange(k)
    return np.exp2(a[idx // 512, idx % 128 // 32])


BF16 = ml_dtypes.bfloat16


def bf(x):
    return np.asarray(x, np.float32).astype(BF16)


def f64(x):
    return np.asarray(x).astype(np.float64)


E2M1 = np.array([0.0, 0.5, 1.0, 1.5, 2.0, 3.0, 4.0, 6.0, -0.0, -0.5, -1.0, -1.5, -2.0, -3.0, -4.0, -6.0])


def pack_weight(w, fmt):
    k, n = w.shape
    w = f64(bf(w)).reshape(k // 32, 32, n)
    amax = np.abs(w).max(1)
    if fmt == "e4m3":
        byte = np.frexp(amax)[1] - 1 + 127 - 7
    else:
        mant, ex = np.frexp(amax / 6.0)
        byte = np.where(mant > 0.5, ex, ex - 1) + 127
    byte = np.clip(np.where(amax > 0, byte, 1), 1, 254)
    scaled = (w * np.exp2(127.0 - byte)[:, None, :]).reshape(k, n).astype(np.float32)
    by_word = np.ascontiguousarray(scaled.reshape(k // 512, 128, 4, n).transpose(0, 1, 3, 2))
    if fmt == "e4m3":
        words = by_word.astype(ml_dtypes.float8_e4m3fn).view(np.uint8)
    else:
        c = by_word.astype(ml_dtypes.float4_e2m1fn).view(np.uint8) & 0xF
        words = c[..., 0::2] | (c[..., 1::2] << 4)
    return np.ascontiguousarray(words), np.ascontiguousarray(byte.astype(np.uint8).reshape(k // 512, 16, n))


def unpack_weight(words, scales, fmt):
    g, p, n, _ = words.shape
    if fmt == "e4m3":
        vals = np.ascontiguousarray(words).view(ml_dtypes.float8_e4m3fn).astype(np.float64)
    else:
        nib = np.empty((g, p, n, 4), np.uint8)
        nib[..., 0::2] = words & 0xF
        nib[..., 1::2] = words >> 4
        vals = E2M1[nib]
    vals = vals * np.repeat(np.exp2(scales.astype(np.float64) - 127.0), 8, axis=1)[..., None]
    return vals.transpose(0, 1, 3, 2).reshape(g * 512, n)


B, NP, H, W, EMB = 4, 1536, 16, 32, 256
L = NP + H * W
C2 = EMB + EMB
BN_EPS = 1e-5


def setup_inputs():
    s = mx_kscale(C2)
    T1 = bf(np.random.standard_normal((B, L, EMB)) * s[:EMB])
    T2 = bf(np.random.standard_normal((B, L, EMB)) * s[EMB:])
    Wf = np.random.standard_normal((EMB, C2)) / np.sqrt(C2) / s[None, :]
    Wf_words, Wf_scales = pack_weight(np.ascontiguousarray(Wf.T), 'e4m3')
    bn_g = bf(1.0 + 0.1 * np.random.standard_normal(EMB))
    bn_b = bf(0.3 * np.random.standard_normal(EMB))
    return {'T1': T1,
            'T2': T2,
            'Wf_words': Wf_words,
            'Wf_scales': Wf_scales,
            'bn_g': bn_g,
            'bn_b': bn_b}


def reference(T1, T2, Wf_words, Wf_scales, bn_g, bn_b):
    joint = np.concatenate([f64(T1).swapaxes(1, 2), f64(T2).swapaxes(1, 2)], axis=1)
    y = unpack_weight(Wf_words, Wf_scales, 'e4m3').T @ mxq(joint, 1, 'e4m3')
    mu = y.mean(axis=(0, 2), keepdims=True)
    var = y.var(axis=(0, 2), keepdims=True)
    y = (y - mu) / np.sqrt(var + BN_EPS)
    y = y * f64(bn_g)[None, :, None] + f64(bn_b)[None, :, None]
    y = np.maximum(y, 0.0)
    return y.swapaxes(1, 2)

@@ -1,0 +1,193 @@
+from contextlib import ExitStack
+
+import concourse.mybir as mybir
+from concourse.masks import make_identity
+
+F32 = mybir.dt.float32
+BF16 = mybir.dt.bfloat16
+I32 = mybir.dt.int32
+U32 = mybir.dt.uint32
+U8 = mybir.dt.uint8
+FP8X4 = mybir.dt.float8_e4m3fn_x4
+ACT = mybir.ActivationFunctionType
+
+P = 128
+ROWS = 4 * 2048
+STREAM = 256
+K = 2 * STREAM
+EMB = 256
+HALVES = EMB // P
+BN_EPS = 1e-5
+
+GROUP = 512
+TILES = GROUP // P
+GROUPS = ROWS // GROUP
+BANK_TILES = 2
+GROUP_BANKS = TILES // BANK_TILES
+RUN = 2
+RUNS = GROUPS // RUN
+
+FLOPS = 2 * ROWS * K * EMB
+
+
+def tile_iag_pb_t_kernel(tc, T1, T2, Wf_words, Wf_scales, bn_g, bn_b, out):
+    nc = tc.nc
+    streams = (T1.flatten_outer_dims(), T2.flatten_outer_dims())
+    out_rows = out.flatten_outer_dims()
+
+    with ExitStack() as ctx:
+        consts = ctx.enter_context(tc.tile_pool(name="consts", bufs=1))
+        x_pool = ctx.enter_context(tc.tile_pool(name="x", bufs=GROUPS))
+        grouped_pool = ctx.enter_context(tc.tile_pool(name="grouped", bufs=2 * RUN))
+        z_pool = ctx.enter_context(tc.tile_pool(name="z", bufs=2 * RUN * HALVES))
+        o_pool = ctx.enter_context(tc.tile_pool(name="o", bufs=2 * RUN))
+        flip_banks = ctx.enter_context(tc.psum_pool(name="flip", bufs=RUN * GROUP_BANKS))
+        y_banks = ctx.enter_context(tc.psum_pool(name="y", bufs=RUN * HALVES))
+        ctx.enter_context(tc.manual_schedule())
+
+        def load_group(g):
+            x_sb = x_pool.tile([P, TILES, K], BF16, name="x_sb")
+            for s in range(2):
+                nc.sync.dma_start(
+                    out=x_sb[:, :, s * STREAM : (s + 1) * STREAM],
+                    in_=streams[s][g * GROUP : (g + 1) * GROUP, :].rearrange("(m j) c -> m j c", j=TILES),
+                )
+            return x_sb
+
+        x_tiles = [load_group(0)]
+
+        w_words = consts.tile([P, EMB], U32, align_bytes=64)
+        nc.sync.dma_start(out=w_words[:].bitcast(I32), in_=Wf_words[0].rearrange("p n t -> p (n t)").bitcast(I32))
+        w_plane = consts.tile([P, EMB], U8, align_bytes=64)
+        nc.vector.memset(w_plane[:].bitcast(I32), 0)
+        for quadrant in range(4):
+            nc.sync.dma_start(
+                out=w_plane[32 * quadrant : 32 * quadrant + 4, :].bitcast(I32),
+                in_=Wf_scales[0, 4 * quadrant : 4 * quadrant + 4, :].bitcast(I32),
+            )
+        for g in range(1, GROUPS):
+            x_tiles.append(load_group(g))
+
+        gb_rows = consts.tile([P, P], BF16)
+        nc.vector.memset(gb_rows[:], 0.0)
+        nc.scalar.dma_start(out=gb_rows[0:HALVES, :], in_=bn_g.rearrange("(h c) -> h c", h=HALVES))
+        nc.scalar.dma_start(out=gb_rows[HALVES : 2 * HALVES, :], in_=bn_b.rearrange("(h c) -> h c", h=HALVES))
+        gb_f32 = consts.tile([P, P], F32)
+        nc.vector.tensor_copy(out=gb_f32[:], in_=gb_rows[:])
+
+        ident = consts.tile([P, P], F32)
+        make_identity(nc, ident[:])
+
+        eps = consts.tile([P, 1], F32)
+        nc.vector.memset(eps[:], BN_EPS)
+        root_of_eps = consts.tile([P, 1], F32)
+        nc.scalar.activation(out=root_of_eps[:], in_=eps[:], func=ACT.Sqrt)
+
+        x_words = consts.tile([P, GROUPS, GROUP], U32, align_bytes=64)
+        x_planes = consts.tile([P, GROUPS, GROUP], U8, align_bytes=64)
+        stats = consts.tile([P, HALVES, GROUPS, 6], F32)
+
+        def flip_group(g):
+            words = x_tiles[g][:].rearrange("m j c -> m (j c)").bitcast(F32)
+            row_words = K // 2
+            grouped = grouped_pool.tile([P, 4 * GROUP], BF16, align_bytes=64, name="grouped")
+            grouped_words = grouped[:].bitcast(F32).rearrange("p (r u) -> p r u", u=2)
+            for b in range(GROUP_BANKS):
+                xt = flip_banks.tile([P, 2, BANK_TILES * P], F32, tag="bank", name="xt")
+                for i in range(BANK_TILES):
+                    j = b * BANK_TILES + i
+                    for u in range(2):
+                        nc.tensor.transpose(
+                            xt[:, u, i * P : (i + 1) * P],
+                            words[:, j * row_words + u : (j + 1) * row_words : 2],
+                            ident[:],
+                        )
+                bank_rows = slice(b * BANK_TILES * P, (b + 1) * BANK_TILES * P)
+                nc.scalar.copy(out=grouped_words[:, bank_rows, :], in_=xt[:].rearrange("p u r -> p r u"))
+            return grouped
+
+        def quantise_group(g, grouped):
+            nc.vector.quantize_mx(out=x_words[:, g, :].bitcast(FP8X4), scales=x_planes[:, g, :], in_=grouped[:])
+
+        def multiply_group(g):
+            banks = []
+            for h in range(HALVES):
+                y = y_banks.tile([P, GROUP], F32, tag="y", name="y")
+                nc.tensor.matmul_mx(
+                    out=y[:],
+                    lhsT=w_words[:, h * P : (h + 1) * P].bitcast(FP8X4),
+                    lhsT_scale=w_plane[:, h * P : (h + 1) * P],
+                    rhs=x_words[:, g, :].bitcast(FP8X4),
+                    rhs_scale=x_planes[:, g, :],
+                    start=True,
+                    stop=True,
+                )
+                banks.append(y)
+            return banks
+
+        def measure_group(g, banks):
+            for h in range(HALVES):
+                nc.vector.bn_stats(out=stats[:, h, g, :], in_=banks[h][:])
+
+        def run_groups(r):
+            return range(r * RUN, (r + 1) * RUN)
+
+        grouped_tiles = {}
+        for r in range(RUNS + 1):
+            if r < RUNS:
+                for g in run_groups(r):
+                    grouped_tiles[g] = flip_group(g)
+            if r > 0:
+                for g in run_groups(r - 1):
+                    measure_group(g, multiply_group(g))
+            if r < RUNS:
+                for g in run_groups(r):
+                    quantise_group(g, grouped_tiles[g])
+
+        mean_var = consts.tile([P, HALVES, 2], F32)
+        for h in range(HALVES):
+            nc.vector.bn_aggr(out=mean_var[:, h, :], in_=stats[:, h, :, :].rearrange("p g s -> p (g s)"))
+        std = consts.tile([P, HALVES], F32)
+        nc.scalar.activation(out=std[:], in_=mean_var[:, :, 1], func=ACT.Sqrt, bias=eps[:])
+        gb_bank = flip_banks.tile([P, 2, BANK_TILES * P], F32, tag="bank", name="gb_bank")
+        nc.tensor.transpose(gb_bank[:, 0, 0:P], gb_f32[:], ident[:])
+        gb_cols = consts.tile([P, 2 * HALVES], F32)
+        nc.vector.tensor_copy(out=gb_cols[:], in_=gb_bank[:, 0, 0 : 2 * HALVES])
+        gain = consts.tile([P, HALVES], F32)
+        nc.vector.reciprocal(out=gain[:], in_=std[:])
+        nc.vector.tensor_mul(out=gain[:], in0=gain[:], in1=gb_cols[:, 0:HALVES])
+        shift = consts.tile([P, HALVES], F32)
+        nc.vector.tensor_mul(out=shift[:], in0=mean_var[:, :, 0], in1=gain[:])
+        nc.vector.tensor_sub(out=shift[:], in0=gb_cols[:, HALVES : 2 * HALVES], in1=shift[:])
+
+        def apply_group(banks):
+            z_tiles = []
+            for h in range(HALVES):
+                z = z_pool.tile([P, GROUP], F32, name="z")
+                nc.scalar.activation(
+                    out=z[:], in_=banks[h][:], func=ACT.Relu, bias=shift[:, h : h + 1], scale=gain[:, h : h + 1]
+                )
+                z_tiles.append(z)
+            return z_tiles
+
+        def unflip_and_store_group(g, z_tiles):
+            o_sb = o_pool.tile([P, TILES, EMB], F32, name="o_sb")
+            for b in range(GROUP_BANKS):
+                ot = flip_banks.tile([P, BANK_TILES, EMB], F32, tag="bank", name="ot")
+                for i in range(BANK_TILES):
+                    j = b * BANK_TILES + i
+                    for h in range(HALVES):
+                        nc.tensor.transpose(ot[:, i, h * P : (h + 1) * P], z_tiles[h][:, j * P : (j + 1) * P], ident[:])
+                nc.vector.tensor_copy(out=o_sb[:, b * BANK_TILES : (b + 1) * BANK_TILES, :], in_=ot[:])
+            nc.sync.dma_start(
+                out=out_rows[g * GROUP : (g + 1) * GROUP, :].rearrange("(m j) n -> m j n", j=TILES), in_=o_sb[:]
+            )
+
+        z_groups = {}
+        for r in range(RUNS + 1):
+            if r < RUNS:
+                for g in run_groups(r):
+                    z_groups[g] = apply_group(multiply_group(g))
+            if r > 0:
+                for g in run_groups(r - 1):
+                    unflip_and_store_group(g, z_groups[g])

@@ -24,8 +24,9 @@ TILES = GROUP // P
 GROUPS = ROWS // GROUP
 BANK_TILES = 2
 GROUP_BANKS = TILES // BANK_TILES
-RUN = 2
+RUN = 1
 RUNS = GROUPS // RUN
+AHEAD = 4
 
 FLOPS = 2 * ROWS * K * EMB
 
@@ -38,11 +39,11 @@ def tile_iag_pb_t_kernel(tc, T1, T2, Wf_words, Wf_scales, bn_g, bn_b, out):
     with ExitStack() as ctx:
         consts = ctx.enter_context(tc.tile_pool(name="consts", bufs=1))
         x_pool = ctx.enter_context(tc.tile_pool(name="x", bufs=GROUPS))
-        grouped_pool = ctx.enter_context(tc.tile_pool(name="grouped", bufs=2 * RUN))
-        z_pool = ctx.enter_context(tc.tile_pool(name="z", bufs=2 * RUN * HALVES))
-        o_pool = ctx.enter_context(tc.tile_pool(name="o", bufs=2 * RUN))
-        flip_banks = ctx.enter_context(tc.psum_pool(name="flip", bufs=RUN * GROUP_BANKS))
-        y_banks = ctx.enter_context(tc.psum_pool(name="y", bufs=RUN * HALVES))
+        grouped_pool = ctx.enter_context(tc.tile_pool(name="grouped", bufs=AHEAD))
+        z_pool = ctx.enter_context(tc.tile_pool(name="z", bufs=AHEAD * HALVES))
+        o_pool = ctx.enter_context(tc.tile_pool(name="o", bufs=AHEAD))
+        flip_banks = ctx.enter_context(tc.psum_pool(name="flip", bufs=4))
+        y_banks = ctx.enter_context(tc.psum_pool(name="y", bufs=4))
         ctx.enter_context(tc.manual_schedule())
 
         def load_group(g):

@@ -10,6 +10,7 @@ U32 = mybir.dt.uint32
 U8 = mybir.dt.uint8
 FP8X4 = mybir.dt.float8_e4m3fn_x4
 ACT = mybir.ActivationFunctionType
+ALU = mybir.AluOpType
 
 P = 128
 ROWS = 4 * 2048
@@ -17,6 +18,8 @@ STREAM = 256
 K = 2 * STREAM
 EMB = 256
 HALVES = EMB // P
+KEPT = 0
+AGAIN = 1
 BN_EPS = 1e-5
 
 GROUP = 512
@@ -24,9 +27,10 @@ TILES = GROUP // P
 GROUPS = ROWS // GROUP
 BANK_TILES = 2
 GROUP_BANKS = TILES // BANK_TILES
-RUN = 1
+RUN = 2
 RUNS = GROUPS // RUN
 AHEAD = 4
+LOOK = 2
 
 FLOPS = 2 * ROWS * K * EMB
 
@@ -40,7 +44,7 @@ def tile_iag_pb_t_kernel(tc, T1, T2, Wf_words, Wf_scales, bn_g, bn_b, out):
         consts = ctx.enter_context(tc.tile_pool(name="consts", bufs=1))
         x_pool = ctx.enter_context(tc.tile_pool(name="x", bufs=GROUPS))
         grouped_pool = ctx.enter_context(tc.tile_pool(name="grouped", bufs=AHEAD))
-        z_pool = ctx.enter_context(tc.tile_pool(name="z", bufs=AHEAD * HALVES))
+        z_pool = ctx.enter_context(tc.tile_pool(name="z", bufs=AHEAD))
         o_pool = ctx.enter_context(tc.tile_pool(name="o", bufs=AHEAD))
         flip_banks = ctx.enter_context(tc.psum_pool(name="flip", bufs=4))
         y_banks = ctx.enter_context(tc.psum_pool(name="y", bufs=4))
@@ -87,6 +91,7 @@ def tile_iag_pb_t_kernel(tc, T1, T2, Wf_words, Wf_scales, bn_g, bn_b, out):
         x_words = consts.tile([P, GROUPS, GROUP], U32, align_bytes=64)
         x_planes = consts.tile([P, GROUPS, GROUP], U8, align_bytes=64)
         stats = consts.tile([P, HALVES, GROUPS, 6], F32)
+        y_kept = consts.tile([P, GROUPS, GROUP], F32)
 
         def flip_group(g):
             words = x_tiles[g][:].rearrange("m j c -> m (j c)").bitcast(F32)
@@ -110,40 +115,46 @@ def tile_iag_pb_t_kernel(tc, T1, T2, Wf_words, Wf_scales, bn_g, bn_b, out):
         def quantise_group(g, grouped):
             nc.vector.quantize_mx(out=x_words[:, g, :].bitcast(FP8X4), scales=x_planes[:, g, :], in_=grouped[:])
 
-        def multiply_group(g):
-            banks = []
-            for h in range(HALVES):
-                y = y_banks.tile([P, GROUP], F32, tag="y", name="y")
-                nc.tensor.matmul_mx(
-                    out=y[:],
-                    lhsT=w_words[:, h * P : (h + 1) * P].bitcast(FP8X4),
-                    lhsT_scale=w_plane[:, h * P : (h + 1) * P],
-                    rhs=x_words[:, g, :].bitcast(FP8X4),
-                    rhs_scale=x_planes[:, g, :],
-                    start=True,
-                    stop=True,
-                )
-                banks.append(y)
-            return banks
+        def multiply(g, h):
+            y = y_banks.tile([P, GROUP], F32, tag="y", name="y")
+            nc.tensor.matmul_mx(
+                out=y[:],
+                lhsT=w_words[:, h * P : (h + 1) * P].bitcast(FP8X4),
+                lhsT_scale=w_plane[:, h * P : (h + 1) * P],
+                rhs=x_words[:, g, :].bitcast(FP8X4),
+                rhs_scale=x_planes[:, g, :],
+                start=True,
+                stop=True,
+            )
+            return y
 
         def measure_group(g, banks):
             for h in range(HALVES):
                 nc.vector.bn_stats(out=stats[:, h, g, :], in_=banks[h][:])
+            nc.scalar.copy(out=y_kept[:, g, :], in_=banks[KEPT][:])
 
         def run_groups(r):
             return range(r * RUN, (r + 1) * RUN)
 
-        grouped_tiles = {}
         for r in range(RUNS + 1):
+            grouped_tiles = {}
+            y_tiles = {}
             if r < RUNS:
                 for g in run_groups(r):
                     grouped_tiles[g] = flip_group(g)
             if r > 0:
                 for g in run_groups(r - 1):
-                    measure_group(g, multiply_group(g))
-            if r < RUNS:
-                for g in run_groups(r):
+                    y_tiles[g] = [multiply(g, h) for h in range(HALVES)]
+            for g in run_groups(r):
+                if r < RUNS:
                     quantise_group(g, grouped_tiles[g])
+                if r > 0:
+                    measure_group(g - RUN, y_tiles[g - RUN])
+
+        again_banks = {}
+        for r in range(min(LOOK, RUNS)):
+            for g in run_groups(r):
+                again_banks[g] = multiply(g, AGAIN)
 
         mean_var = consts.tile([P, HALVES, 2], F32)
         for h in range(HALVES):
@@ -161,34 +172,51 @@ def tile_iag_pb_t_kernel(tc, T1, T2, Wf_words, Wf_scales, bn_g, bn_b, out):
         nc.vector.tensor_mul(out=shift[:], in0=mean_var[:, :, 0], in1=gain[:])
         nc.vector.tensor_sub(out=shift[:], in0=gb_cols[:, HALVES : 2 * HALVES], in1=shift[:])
 
-        def apply_group(banks):
-            z_tiles = []
-            for h in range(HALVES):
-                z = z_pool.tile([P, GROUP], F32, name="z")
-                nc.scalar.activation(
-                    out=z[:], in_=banks[h][:], func=ACT.Relu, bias=shift[:, h : h + 1], scale=gain[:, h : h + 1]
-                )
-                z_tiles.append(z)
-            return z_tiles
+        def apply_group(g):
+            nc.gpsimd.tensor_scalar(
+                out=y_kept[:, g, :],
+                in0=y_kept[:, g, :],
+                scalar1=gain[:, KEPT : KEPT + 1],
+                scalar2=shift[:, KEPT : KEPT + 1],
+                op0=ALU.mult,
+                op1=ALU.add,
+            )
+            z = z_pool.tile([P, GROUP], F32, name="z")
+            nc.scalar.activation(
+                out=z[:],
+                in_=again_banks[g][:],
+                func=ACT.Identity,
+                bias=shift[:, AGAIN : AGAIN + 1],
+                scale=gain[:, AGAIN : AGAIN + 1],
+            )
+            return {KEPT: y_kept[:, g, :], AGAIN: z[:]}
 
-        def unflip_and_store_group(g, z_tiles):
+        def unflip_and_store_group(g, halves):
             o_sb = o_pool.tile([P, TILES, EMB], F32, name="o_sb")
             for b in range(GROUP_BANKS):
                 ot = flip_banks.tile([P, BANK_TILES, EMB], F32, tag="bank", name="ot")
                 for i in range(BANK_TILES):
                     j = b * BANK_TILES + i
                     for h in range(HALVES):
-                        nc.tensor.transpose(ot[:, i, h * P : (h + 1) * P], z_tiles[h][:, j * P : (j + 1) * P], ident[:])
-                nc.vector.tensor_copy(out=o_sb[:, b * BANK_TILES : (b + 1) * BANK_TILES, :], in_=ot[:])
+                        nc.tensor.transpose(ot[:, i, h * P : (h + 1) * P], halves[h][:, j * P : (j + 1) * P], ident[:])
+                o_rows = o_sb[:, b * BANK_TILES : (b + 1) * BANK_TILES, :]
+                if g % 2 == 1 and b == GROUP_BANKS - 1:
+                    nc.scalar.activation(out=o_rows, in_=ot[:], func=ACT.Relu)
+                else:
+                    nc.vector.tensor_scalar_max(out=o_rows, in0=ot[:], scalar1=0.0)
             nc.sync.dma_start(
                 out=out_rows[g * GROUP : (g + 1) * GROUP, :].rearrange("(m j) n -> m j n", j=TILES), in_=o_sb[:]
             )
 
-        z_groups = {}
-        for r in range(RUNS + 1):
-            if r < RUNS:
-                for g in run_groups(r):
-                    z_groups[g] = apply_group(multiply_group(g))
-            if r > 0:
-                for g in run_groups(r - 1):
-                    unflip_and_store_group(g, z_groups[g])
+        applied = {}
+        for g in run_groups(0):
+            applied[g] = apply_group(g)
+        for r in range(RUNS):
+            if r + LOOK < RUNS:
+                for g in run_groups(r + LOOK):
+                    again_banks[g] = multiply(g, AGAIN)
+            if r + 1 < RUNS:
+                for g in run_groups(r + 1):
+                    applied[g] = apply_group(g)
+            for g in run_groups(r):
+                unflip_and_store_group(g, applied[g])

@@ -145,11 +145,12 @@ def tile_iag_pb_t_kernel(tc, T1, T2, Wf_words, Wf_scales, bn_g, bn_b, out):
             if r > 0:
                 for g in run_groups(r - 1):
                     y_tiles[g] = [multiply(g, h) for h in range(HALVES)]
-            for g in run_groups(r):
-                if r < RUNS:
+            if r > 0:
+                for g in run_groups(r - 1):
+                    measure_group(g, y_tiles[g])
+            if r < RUNS:
+                for g in run_groups(r):
                     quantise_group(g, grouped_tiles[g])
-                if r > 0:
-                    measure_group(g - RUN, y_tiles[g - RUN])
 
         again_banks = {}
         for r in range(min(LOOK, RUNS)):

@@ -29,7 +29,7 @@ BANK_TILES = 2
 GROUP_BANKS = TILES // BANK_TILES
 RUN = 2
 RUNS = GROUPS // RUN
-AHEAD = 4
+AHEAD = 8
 LOOK = 2
 
 FLOPS = 2 * ROWS * K * EMB

@@ -30,7 +30,7 @@ GROUP_BANKS = TILES // BANK_TILES
 RUN = 2
 RUNS = GROUPS // RUN
 AHEAD = 8
-LOOK = 2
+STAY = GROUPS - 4
 
 FLOPS = 2 * ROWS * K * EMB
 
@@ -46,8 +46,7 @@ def tile_iag_pb_t_kernel(tc, T1, T2, Wf_words, Wf_scales, bn_g, bn_b, out):
         grouped_pool = ctx.enter_context(tc.tile_pool(name="grouped", bufs=AHEAD))
         z_pool = ctx.enter_context(tc.tile_pool(name="z", bufs=AHEAD))
         o_pool = ctx.enter_context(tc.tile_pool(name="o", bufs=AHEAD))
-        flip_banks = ctx.enter_context(tc.psum_pool(name="flip", bufs=4))
-        y_banks = ctx.enter_context(tc.psum_pool(name="y", bufs=4))
+        banks = ctx.enter_context(tc.psum_pool(name="banks", bufs=8))
         ctx.enter_context(tc.manual_schedule())
 
         def load_group(g):
@@ -99,7 +98,7 @@ def tile_iag_pb_t_kernel(tc, T1, T2, Wf_words, Wf_scales, bn_g, bn_b, out):
             grouped = grouped_pool.tile([P, 4 * GROUP], BF16, align_bytes=64, name="grouped")
             grouped_words = grouped[:].bitcast(F32).rearrange("p (r u) -> p r u", u=2)
             for b in range(GROUP_BANKS):
-                xt = flip_banks.tile([P, 2, BANK_TILES * P], F32, tag="bank", name="xt")
+                xt = banks.tile([P, 2, BANK_TILES * P], F32, tag="bank", name="xt")
                 for i in range(BANK_TILES):
                     j = b * BANK_TILES + i
                     for u in range(2):
@@ -116,7 +115,7 @@ def tile_iag_pb_t_kernel(tc, T1, T2, Wf_words, Wf_scales, bn_g, bn_b, out):
             nc.vector.quantize_mx(out=x_words[:, g, :].bitcast(FP8X4), scales=x_planes[:, g, :], in_=grouped[:])
 
         def multiply(g, h):
-            y = y_banks.tile([P, GROUP], F32, tag="y", name="y")
+            y = banks.tile([P, GROUP], F32, tag="bank", name="y")
             nc.tensor.matmul_mx(
                 out=y[:],
                 lhsT=w_words[:, h * P : (h + 1) * P].bitcast(FP8X4),
@@ -128,20 +127,26 @@ def tile_iag_pb_t_kernel(tc, T1, T2, Wf_words, Wf_scales, bn_g, bn_b, out):
             )
             return y
 
-        def measure_group(g, banks):
+        def measure_group(g, products):
             for h in range(HALVES):
-                nc.vector.bn_stats(out=stats[:, h, g, :], in_=banks[h][:])
-            nc.scalar.copy(out=y_kept[:, g, :], in_=banks[KEPT][:])
+                nc.vector.bn_stats(out=stats[:, h, g, :], in_=products[h][:])
+            if g != STAY:
+                nc.scalar.copy(out=y_kept[:, g, :], in_=products[KEPT][:])
 
         def run_groups(r):
             return range(r * RUN, (r + 1) * RUN)
 
+        y_tiles = {}
+        gb_cols = consts.tile([P, 2 * HALVES], F32)
         for r in range(RUNS + 1):
             grouped_tiles = {}
-            y_tiles = {}
             if r < RUNS:
                 for g in run_groups(r):
                     grouped_tiles[g] = flip_group(g)
+            if r == 0:
+                gb_bank = banks.tile([P, 2, BANK_TILES * P], F32, tag="bank", name="gb_bank")
+                nc.tensor.transpose(gb_bank[:, 0, 0:P], gb_f32[:], ident[:])
+                nc.vector.tensor_copy(out=gb_cols[:], in_=gb_bank[:, 0, 0 : 2 * HALVES])
             if r > 0:
                 for g in run_groups(r - 1):
                     y_tiles[g] = [multiply(g, h) for h in range(HALVES)]
@@ -152,20 +157,11 @@ def tile_iag_pb_t_kernel(tc, T1, T2, Wf_words, Wf_scales, bn_g, bn_b, out):
                 for g in run_groups(r):
                     quantise_group(g, grouped_tiles[g])
 
-        again_banks = {}
-        for r in range(min(LOOK, RUNS)):
-            for g in run_groups(r):
-                again_banks[g] = multiply(g, AGAIN)
-
         mean_var = consts.tile([P, HALVES, 2], F32)
         for h in range(HALVES):
             nc.vector.bn_aggr(out=mean_var[:, h, :], in_=stats[:, h, :, :].rearrange("p g s -> p (g s)"))
         std = consts.tile([P, HALVES], F32)
         nc.scalar.activation(out=std[:], in_=mean_var[:, :, 1], func=ACT.Sqrt, bias=eps[:])
-        gb_bank = flip_banks.tile([P, 2, BANK_TILES * P], F32, tag="bank", name="gb_bank")
-        nc.tensor.transpose(gb_bank[:, 0, 0:P], gb_f32[:], ident[:])
-        gb_cols = consts.tile([P, 2 * HALVES], F32)
-        nc.vector.tensor_copy(out=gb_cols[:], in_=gb_bank[:, 0, 0 : 2 * HALVES])
         gain = consts.tile([P, HALVES], F32)
         nc.vector.reciprocal(out=gain[:], in_=std[:])
         nc.vector.tensor_mul(out=gain[:], in0=gain[:], in1=gb_cols[:, 0:HALVES])
@@ -173,7 +169,29 @@ def tile_iag_pb_t_kernel(tc, T1, T2, Wf_words, Wf_scales, bn_g, bn_b, out):
         nc.vector.tensor_mul(out=shift[:], in0=mean_var[:, :, 0], in1=gain[:])
         nc.vector.tensor_sub(out=shift[:], in0=gb_cols[:, HALVES : 2 * HALVES], in1=shift[:])
 
+        def apply_from_bank(engine, bank, h):
+            z = z_pool.tile([P, GROUP], F32, name="z")
+            if engine == "scalar":
+                nc.scalar.activation(
+                    out=z[:], in_=bank[:], func=ACT.Identity, bias=shift[:, h : h + 1], scale=gain[:, h : h + 1]
+                )
+            else:
+                nc.vector.tensor_scalar(
+                    out=z[:],
+                    in0=bank[:],
+                    scalar1=gain[:, h : h + 1],
+                    scalar2=shift[:, h : h + 1],
+                    op0=ALU.mult,
+                    op1=ALU.add,
+                )
+            return z[:]
+
         def apply_group(g):
+            if g == STAY:
+                return {
+                    KEPT: apply_from_bank("scalar", y_tiles[g][KEPT], KEPT),
+                    AGAIN: apply_from_bank("vector", y_tiles[g][AGAIN], AGAIN),
+                }
             nc.gpsimd.tensor_scalar(
                 out=y_kept[:, g, :],
                 in0=y_kept[:, g, :],
@@ -182,26 +200,18 @@ def tile_iag_pb_t_kernel(tc, T1, T2, Wf_words, Wf_scales, bn_g, bn_b, out):
                 op0=ALU.mult,
                 op1=ALU.add,
             )
-            z = z_pool.tile([P, GROUP], F32, name="z")
-            nc.scalar.activation(
-                out=z[:],
-                in_=again_banks[g][:],
-                func=ACT.Identity,
-                bias=shift[:, AGAIN : AGAIN + 1],
-                scale=gain[:, AGAIN : AGAIN + 1],
-            )
-            return {KEPT: y_kept[:, g, :], AGAIN: z[:]}
+            return {KEPT: y_kept[:, g, :], AGAIN: apply_from_bank("scalar", y_tiles[g][AGAIN], AGAIN)}
 
-        def unflip_and_store_group(g, halves):
+        def unflip_and_store_group(g, halves, scalar_banks):
             o_sb = o_pool.tile([P, TILES, EMB], F32, name="o_sb")
             for b in range(GROUP_BANKS):
-                ot = flip_banks.tile([P, BANK_TILES, EMB], F32, tag="bank", name="ot")
+                ot = banks.tile([P, BANK_TILES, EMB], F32, tag="bank", name="ot")
                 for i in range(BANK_TILES):
                     j = b * BANK_TILES + i
                     for h in range(HALVES):
                         nc.tensor.transpose(ot[:, i, h * P : (h + 1) * P], halves[h][:, j * P : (j + 1) * P], ident[:])
                 o_rows = o_sb[:, b * BANK_TILES : (b + 1) * BANK_TILES, :]
-                if g % 2 == 1 and b == GROUP_BANKS - 1:
+                if b in scalar_banks:
                     nc.scalar.activation(out=o_rows, in_=ot[:], func=ACT.Relu)
                 else:
                     nc.vector.tensor_scalar_max(out=o_rows, in0=ot[:], scalar1=0.0)
@@ -209,15 +219,21 @@ def tile_iag_pb_t_kernel(tc, T1, T2, Wf_words, Wf_scales, bn_g, bn_b, out):
                 out=out_rows[g * GROUP : (g + 1) * GROUP, :].rearrange("(m j) n -> m j n", j=TILES), in_=o_sb[:]
             )
 
+        order = list(range(STAY, GROUPS)) + list(range(STAY))
+        runs = [order[i : i + RUN] for i in range(0, GROUPS, RUN)]
         applied = {}
-        for g in run_groups(0):
-            applied[g] = apply_group(g)
-        for r in range(RUNS):
-            if r + LOOK < RUNS:
-                for g in run_groups(r + LOOK):
-                    again_banks[g] = multiply(g, AGAIN)
-            if r + 1 < RUNS:
-                for g in run_groups(r + 1):
+        first = runs[0]
+        applied[first[0]] = apply_group(first[0])
+        applied[first[1]] = apply_group(first[1])
+        unflip_and_store_group(first[0], applied[first[0]], (1,))
+        applied[runs[1][0]] = apply_group(runs[1][0])
+        unflip_and_store_group(first[1], applied[first[1]], ())
+        applied[runs[1][1]] = apply_group(runs[1][1])
+        for i in range(1, RUNS):
+            if i + 1 < RUNS:
+                for g in runs[i + 1]:
+                    y_tiles[g][AGAIN] = multiply(g, AGAIN)
+                for g in runs[i + 1]:
                     applied[g] = apply_group(g)
-            for g in run_groups(r):
-                unflip_and_store_group(g, applied[g])
+            unflip_and_store_group(runs[i][0], applied[runs[i][0]], ())
+            unflip_and_store_group(runs[i][1], applied[runs[i][1]], (1,))

@@ -30,7 +30,9 @@ GROUP_BANKS = TILES // BANK_TILES
 RUN = 2
 RUNS = GROUPS // RUN
 AHEAD = 8
-STAY = GROUPS - 4
+BOTH_KEPT = (GROUPS - 4, GROUPS - 3)
+S_MEASURED = BOTH_KEPT
+FIRST = GROUPS - 2
 
 FLOPS = 2 * ROWS * K * EMB
 
@@ -89,8 +91,13 @@ def tile_iag_pb_t_kernel(tc, T1, T2, Wf_words, Wf_scales, bn_g, bn_b, out):
 
         x_words = consts.tile([P, GROUPS, GROUP], U32, align_bytes=64)
         x_planes = consts.tile([P, GROUPS, GROUP], U8, align_bytes=64)
-        stats = consts.tile([P, HALVES, GROUPS, 6], F32)
+        stats = consts.tile([P, HALVES, 2 * GROUPS, 3], F32)
+        nc.vector.memset(stats[:, KEPT, 0 : len(S_MEASURED), 0:1], float(GROUP))
+        used = {KEPT: len(S_MEASURED), AGAIN: 0}
+        sums = consts.tile([P, len(S_MEASURED)], F32)
+        squares = consts.tile([P, GROUP], F32)
         y_kept = consts.tile([P, GROUPS, GROUP], F32)
+        y_more = consts.tile([P, len(BOTH_KEPT), GROUP], F32)
 
         def flip_group(g):
             words = x_tiles[g][:].rearrange("m j c -> m (j c)").bitcast(F32)
@@ -129,9 +136,29 @@ def tile_iag_pb_t_kernel(tc, T1, T2, Wf_words, Wf_scales, bn_g, bn_b, out):
 
         def measure_group(g, products):
             for h in range(HALVES):
-                nc.vector.bn_stats(out=stats[:, h, g, :], in_=products[h][:])
-            if g != STAY:
+                if h == AGAIN or g not in S_MEASURED:
+                    nc.vector.bn_stats(
+                        out=stats[:, h, used[h] : used[h] + 2, :].rearrange("p t s -> p (t s)"), in_=products[h][:]
+                    )
+                    used[h] = used[h] + 2
+            if g in S_MEASURED:
+                i = S_MEASURED.index(g)
+                nc.scalar.activation(
+                    out=y_kept[:, g, :], in_=products[KEPT][:], func=ACT.Identity, accum_out=sums[:, i : i + 1]
+                )
+                nc.scalar.mul(out=stats[:, KEPT, i, 1:2], in_=sums[:, i : i + 1], mul=1.0 / GROUP)
+                nc.scalar.activation(
+                    out=squares[:],
+                    in_=products[KEPT][:],
+                    func=ACT.Square,
+                    scale=-1.0,
+                    bias=stats[:, KEPT, i, 1:2],
+                    accum_out=stats[:, KEPT, i, 2:3],
+                )
+            elif g != FIRST:
                 nc.scalar.copy(out=y_kept[:, g, :], in_=products[KEPT][:])
+            if g in BOTH_KEPT:
+                nc.scalar.copy(out=y_more[:, BOTH_KEPT.index(g), :], in_=products[AGAIN][:])
 
         def run_groups(r):
             return range(r * RUN, (r + 1) * RUN)
@@ -157,9 +184,13 @@ def tile_iag_pb_t_kernel(tc, T1, T2, Wf_words, Wf_scales, bn_g, bn_b, out):
                 for g in run_groups(r):
                     quantise_group(g, grouped_tiles[g])
 
+        order = [FIRST, FIRST + 1] + list(range(FIRST))
+        for g in order[2:6]:
+            y_tiles[g][AGAIN] = multiply(g, AGAIN)
+
         mean_var = consts.tile([P, HALVES, 2], F32)
         for h in range(HALVES):
-            nc.vector.bn_aggr(out=mean_var[:, h, :], in_=stats[:, h, :, :].rearrange("p g s -> p (g s)"))
+            nc.vector.bn_aggr(out=mean_var[:, h, :], in_=stats[:, h, 0 : used[h], :].rearrange("p t s -> p (t s)"))
         std = consts.tile([P, HALVES], F32)
         nc.scalar.activation(out=std[:], in_=mean_var[:, :, 1], func=ACT.Sqrt, bias=eps[:])
         gain = consts.tile([P, HALVES], F32)
@@ -186,21 +217,27 @@ def tile_iag_pb_t_kernel(tc, T1, T2, Wf_words, Wf_scales, bn_g, bn_b, out):
                 )
             return z[:]
 
-        def apply_group(g):
-            if g == STAY:
+        def apply_in_place(y):
+            nc.gpsimd.tensor_scalar(
+                out=y[0], in0=y[0], scalar1=gain[:, y[1] : y[1] + 1], scalar2=shift[:, y[1] : y[1] + 1], op0=ALU.mult, op1=ALU.add
+            )
+            return y[0]
+
+        def apply_group(g, engine):
+            if g == FIRST:
                 return {
                     KEPT: apply_from_bank("scalar", y_tiles[g][KEPT], KEPT),
                     AGAIN: apply_from_bank("vector", y_tiles[g][AGAIN], AGAIN),
                 }
-            nc.gpsimd.tensor_scalar(
-                out=y_kept[:, g, :],
-                in0=y_kept[:, g, :],
-                scalar1=gain[:, KEPT : KEPT + 1],
-                scalar2=shift[:, KEPT : KEPT + 1],
-                op0=ALU.mult,
-                op1=ALU.add,
-            )
-            return {KEPT: y_kept[:, g, :], AGAIN: apply_from_bank("scalar", y_tiles[g][AGAIN], AGAIN)}
+            if g in BOTH_KEPT:
+                return {
+                    KEPT: apply_in_place((y_kept[:, g, :], KEPT)),
+                    AGAIN: apply_in_place((y_more[:, BOTH_KEPT.index(g), :], AGAIN)),
+                }
+            return {
+                KEPT: apply_in_place((y_kept[:, g, :], KEPT)),
+                AGAIN: apply_from_bank(engine, y_tiles[g][AGAIN], AGAIN),
+            }
 
         def unflip_and_store_group(g, halves, scalar_banks):
             o_sb = o_pool.tile([P, TILES, EMB], F32, name="o_sb")
@@ -219,21 +256,16 @@ def tile_iag_pb_t_kernel(tc, T1, T2, Wf_words, Wf_scales, bn_g, bn_b, out):
                 out=out_rows[g * GROUP : (g + 1) * GROUP, :].rearrange("(m j) n -> m j n", j=TILES), in_=o_sb[:]
             )
 
-        order = list(range(STAY, GROUPS)) + list(range(STAY))
-        runs = [order[i : i + RUN] for i in range(0, GROUPS, RUN)]
+        ahead = 3
+        engines = ("vector", "scalar")
         applied = {}
-        first = runs[0]
-        applied[first[0]] = apply_group(first[0])
-        applied[first[1]] = apply_group(first[1])
-        unflip_and_store_group(first[0], applied[first[0]], (1,))
-        applied[runs[1][0]] = apply_group(runs[1][0])
-        unflip_and_store_group(first[1], applied[first[1]], ())
-        applied[runs[1][1]] = apply_group(runs[1][1])
-        for i in range(1, RUNS):
-            if i + 1 < RUNS:
-                for g in runs[i + 1]:
-                    y_tiles[g][AGAIN] = multiply(g, AGAIN)
-                for g in runs[i + 1]:
-                    applied[g] = apply_group(g)
-            unflip_and_store_group(runs[i][0], applied[runs[i][0]], ())
-            unflip_and_store_group(runs[i][1], applied[runs[i][1]], (1,))
+        for n in range(ahead):
+            applied[order[n]] = apply_group(order[n], engines[n % 2])
+        for n in range(GROUPS):
+            unflip_and_store_group(order[n], applied[order[n]], (1,))
+            if n % 2 == 1 and n >= 3:
+                for g in order[n + ahead : n + ahead + 2]:
+                    if g not in BOTH_KEPT:
+                        y_tiles[g][AGAIN] = multiply(g, AGAIN)
+            if n + ahead < GROUPS:
+                applied[order[n + ahead]] = apply_group(order[n + ahead], engines[(n + ahead) % 2])

@@ -160,28 +160,25 @@ def tile_iag_pb_t_kernel(tc, T1, T2, Wf_words, Wf_scales, bn_g, bn_b, out):
             if g in BOTH_KEPT:
                 nc.scalar.copy(out=y_more[:, BOTH_KEPT.index(g), :], in_=products[AGAIN][:])
 
-        def run_groups(r):
-            return range(r * RUN, (r + 1) * RUN)
-
+        part_one_runs = [[0], [1]] + [[g, g + 1] for g in range(2, GROUPS, RUN)]
         y_tiles = {}
         gb_cols = consts.tile([P, 2 * HALVES], F32)
-        for r in range(RUNS + 1):
+        for r in range(len(part_one_runs) + 1):
             grouped_tiles = {}
-            if r < RUNS:
-                for g in run_groups(r):
+            if r < len(part_one_runs):
+                for g in part_one_runs[r]:
                     grouped_tiles[g] = flip_group(g)
             if r == 0:
                 gb_bank = banks.tile([P, 2, BANK_TILES * P], F32, tag="bank", name="gb_bank")
                 nc.tensor.transpose(gb_bank[:, 0, 0:P], gb_f32[:], ident[:])
                 nc.vector.tensor_copy(out=gb_cols[:], in_=gb_bank[:, 0, 0 : 2 * HALVES])
             if r > 0:
-                for g in run_groups(r - 1):
+                for g in part_one_runs[r - 1]:
                     y_tiles[g] = [multiply(g, h) for h in range(HALVES)]
-            if r > 0:
-                for g in run_groups(r - 1):
+                for g in part_one_runs[r - 1]:
                     measure_group(g, y_tiles[g])
-            if r < RUNS:
-                for g in run_groups(r):
+            if r < len(part_one_runs):
+                for g in part_one_runs[r]:
                     quantise_group(g, grouped_tiles[g])
 
         order = [FIRST, FIRST + 1] + list(range(FIRST))

@@ -32,6 +32,7 @@ RUNS = GROUPS // RUN
 AHEAD = 8
 BOTH_KEPT = (GROUPS - 4, GROUPS - 3)
 S_MEASURED = BOTH_KEPT
+PAIRS_BY_GROUP = 2
 FIRST = GROUPS - 2
 
 FLOPS = 2 * ROWS * K * EMB
@@ -44,21 +45,35 @@ def tile_iag_pb_t_kernel(tc, T1, T2, Wf_words, Wf_scales, bn_g, bn_b, out):
 
     with ExitStack() as ctx:
         consts = ctx.enter_context(tc.tile_pool(name="consts", bufs=1))
-        x_pool = ctx.enter_context(tc.tile_pool(name="x", bufs=GROUPS))
+        x_pool = ctx.enter_context(tc.tile_pool(name="x", bufs=GROUPS // 2))
         grouped_pool = ctx.enter_context(tc.tile_pool(name="grouped", bufs=AHEAD))
         z_pool = ctx.enter_context(tc.tile_pool(name="z", bufs=AHEAD))
         o_pool = ctx.enter_context(tc.tile_pool(name="o", bufs=AHEAD))
         banks = ctx.enter_context(tc.psum_pool(name="banks", bufs=8))
         ctx.enter_context(tc.manual_schedule())
 
-        def load_group(g):
-            x_sb = x_pool.tile([P, TILES, K], BF16, name="x_sb")
+        pair_tiles = {}
+
+        def load_places(r, places):
             for s in range(2):
                 nc.sync.dma_start(
-                    out=x_sb[:, :, s * STREAM : (s + 1) * STREAM],
-                    in_=streams[s][g * GROUP : (g + 1) * GROUP, :].rearrange("(m j) c -> m j c", j=TILES),
+                    out=pair_tiles[r][:, places, s * STREAM : (s + 1) * STREAM],
+                    in_=streams[s][r * 2 * GROUP : (r + 1) * 2 * GROUP, :].rearrange("(m j) c -> m j c", j=2 * TILES)[
+                        :, places, :
+                    ],
                 )
-            return x_sb
+
+        def load_group(g):
+            r = g // 2
+            places = slice((g % 2) * TILES, (g % 2 + 1) * TILES)
+            if g % 2 == 0:
+                x_pair = x_pool.tile([P, 2 * TILES, K], BF16, name="x_pair")
+                pair_tiles[r] = x_pair
+            if r < PAIRS_BY_GROUP:
+                load_places(r, places)
+            elif g % 2 == 0:
+                load_places(r, slice(0, 2 * TILES))
+            return pair_tiles[r][:, places, :]
 
         x_tiles = [load_group(0)]
 
@@ -100,7 +115,7 @@ def tile_iag_pb_t_kernel(tc, T1, T2, Wf_words, Wf_scales, bn_g, bn_b, out):
         y_more = consts.tile([P, len(BOTH_KEPT), GROUP], F32)
 
         def flip_group(g):
-            words = x_tiles[g][:].rearrange("m j c -> m (j c)").bitcast(F32)
+            words = x_tiles[g].rearrange("m j c -> m (j c)").bitcast(F32)
             row_words = K // 2
             grouped = grouped_pool.tile([P, 4 * GROUP], BF16, align_bytes=64, name="grouped")
             grouped_words = grouped[:].bitcast(F32).rearrange("p (r u) -> p r u", u=2)
@@ -197,21 +212,27 @@ def tile_iag_pb_t_kernel(tc, T1, T2, Wf_words, Wf_scales, bn_g, bn_b, out):
         nc.vector.tensor_mul(out=shift[:], in0=mean_var[:, :, 0], in1=gain[:])
         nc.vector.tensor_sub(out=shift[:], in0=gb_cols[:, HALVES : 2 * HALVES], in1=shift[:])
 
-        def apply_from_bank(engine, bank, h):
+        def apply_from_bank(engine, bank, h, pieces=1):
             z = z_pool.tile([P, GROUP], F32, name="z")
-            if engine == "scalar":
-                nc.scalar.activation(
-                    out=z[:], in_=bank[:], func=ACT.Identity, bias=shift[:, h : h + 1], scale=gain[:, h : h + 1]
-                )
-            else:
-                nc.vector.tensor_scalar(
-                    out=z[:],
-                    in0=bank[:],
-                    scalar1=gain[:, h : h + 1],
-                    scalar2=shift[:, h : h + 1],
-                    op0=ALU.mult,
-                    op1=ALU.add,
-                )
+            for piece in range(pieces):
+                cols = slice(piece * GROUP // pieces, (piece + 1) * GROUP // pieces)
+                if engine == "scalar":
+                    nc.scalar.activation(
+                        out=z[:, cols],
+                        in_=bank[:, cols],
+                        func=ACT.Identity,
+                        bias=shift[:, h : h + 1],
+                        scale=gain[:, h : h + 1],
+                    )
+                else:
+                    nc.vector.tensor_scalar(
+                        out=z[:, cols],
+                        in0=bank[:, cols],
+                        scalar1=gain[:, h : h + 1],
+                        scalar2=shift[:, h : h + 1],
+                        op0=ALU.mult,
+                        op1=ALU.add,
+                    )
             return z[:]
 
         def apply_in_place(y):
@@ -223,8 +244,8 @@ def tile_iag_pb_t_kernel(tc, T1, T2, Wf_words, Wf_scales, bn_g, bn_b, out):
         def apply_group(g, engine):
             if g == FIRST:
                 return {
-                    KEPT: apply_from_bank("scalar", y_tiles[g][KEPT], KEPT),
-                    AGAIN: apply_from_bank("vector", y_tiles[g][AGAIN], AGAIN),
+                    KEPT: apply_from_bank("scalar", y_tiles[g][KEPT], KEPT, pieces=GROUP_BANKS),
+                    AGAIN: apply_from_bank("vector", y_tiles[g][AGAIN], AGAIN, pieces=GROUP_BANKS),
                 }
             if g in BOTH_KEPT:
                 return {
@@ -235,6 +256,12 @@ def tile_iag_pb_t_kernel(tc, T1, T2, Wf_words, Wf_scales, bn_g, bn_b, out):
                 KEPT: apply_in_place((y_kept[:, g, :], KEPT)),
                 AGAIN: apply_from_bank(engine, y_tiles[g][AGAIN], AGAIN),
             }
+
+        def group_rows(g):
+            pair_rows = out_rows[(g // 2) * 2 * GROUP : (g // 2 + 1) * 2 * GROUP, :].rearrange(
+                "(m j) n -> m j n", j=2 * TILES
+            )
+            return pair_rows[:, (g % 2) * TILES : (g % 2 + 1) * TILES, :]
 
         def unflip_and_store_group(g, halves, scalar_banks):
             o_sb = o_pool.tile([P, TILES, EMB], F32, name="o_sb")
@@ -249,9 +276,17 @@ def tile_iag_pb_t_kernel(tc, T1, T2, Wf_words, Wf_scales, bn_g, bn_b, out):
                     nc.scalar.activation(out=o_rows, in_=ot[:], func=ACT.Relu)
                 else:
                     nc.vector.tensor_scalar_max(out=o_rows, in0=ot[:], scalar1=0.0)
-            nc.sync.dma_start(
-                out=out_rows[g * GROUP : (g + 1) * GROUP, :].rearrange("(m j) n -> m j n", j=TILES), in_=o_sb[:]
-            )
+                if g == FIRST:
+                    nc.sync.dma_start(
+                        out=group_rows(g)[
+                            :, b * BANK_TILES : (b + 1) * BANK_TILES, :
+                        ],
+                        in_=o_rows,
+                    )
+            if g != FIRST:
+                nc.sync.dma_start(
+                    out=group_rows(g), in_=o_sb[:]
+                )
 
         ahead = 3
         engines = ("vector", "scalar")

@@ -178,7 +178,8 @@ def tile_iag_pb_t_kernel(tc, T1, T2, Wf_words, Wf_scales, bn_g, bn_b, out):
         part_one_runs = [[0], [1]] + [[g, g + 1] for g in range(2, GROUPS, RUN)]
         y_tiles = {}
         gb_cols = consts.tile([P, 2 * HALVES], F32)
-        for r in range(len(part_one_runs) + 1):
+        lag = 2
+        for r in range(len(part_one_runs) + lag):
             grouped_tiles = {}
             if r < len(part_one_runs):
                 for g in part_one_runs[r]:
@@ -187,10 +188,10 @@ def tile_iag_pb_t_kernel(tc, T1, T2, Wf_words, Wf_scales, bn_g, bn_b, out):
                 gb_bank = banks.tile([P, 2, BANK_TILES * P], F32, tag="bank", name="gb_bank")
                 nc.tensor.transpose(gb_bank[:, 0, 0:P], gb_f32[:], ident[:])
                 nc.vector.tensor_copy(out=gb_cols[:], in_=gb_bank[:, 0, 0 : 2 * HALVES])
-            if r > 0:
-                for g in part_one_runs[r - 1]:
+            if r >= lag:
+                for g in part_one_runs[r - lag]:
                     y_tiles[g] = [multiply(g, h) for h in range(HALVES)]
-                for g in part_one_runs[r - 1]:
+                for g in part_one_runs[r - lag]:
                     measure_group(g, y_tiles[g])
             if r < len(part_one_runs):
                 for g in part_one_runs[r]:

@@ -206,12 +206,23 @@ def tile_iag_pb_t_kernel(tc, T1, T2, Wf_words, Wf_scales, bn_g, bn_b, out):
             nc.vector.bn_aggr(out=mean_var[:, h, :], in_=stats[:, h, 0 : used[h], :].rearrange("p t s -> p (t s)"))
         std = consts.tile([P, HALVES], F32)
         nc.scalar.activation(out=std[:], in_=mean_var[:, :, 1], func=ACT.Sqrt, bias=eps[:])
+        minus_mean_g = consts.tile([P, HALVES], F32)
+        nc.vector.tensor_mul(out=minus_mean_g[:], in0=mean_var[:, :, 0], in1=gb_cols[:, 0:HALVES])
+        nc.vector.tensor_scalar_mul(out=minus_mean_g[:], in0=minus_mean_g[:], scalar1=-1.0)
+        one_over_std = consts.tile([P, HALVES], F32)
+        nc.vector.reciprocal(out=one_over_std[:], in_=std[:])
         gain = consts.tile([P, HALVES], F32)
-        nc.vector.reciprocal(out=gain[:], in_=std[:])
-        nc.vector.tensor_mul(out=gain[:], in0=gain[:], in1=gb_cols[:, 0:HALVES])
         shift = consts.tile([P, HALVES], F32)
-        nc.vector.tensor_mul(out=shift[:], in0=mean_var[:, :, 0], in1=gain[:])
-        nc.vector.tensor_sub(out=shift[:], in0=gb_cols[:, HALVES : 2 * HALVES], in1=shift[:])
+        nc.vector.tensor_mul(out=gain[:], in0=one_over_std[:], in1=gb_cols[:, 0:HALVES])
+        for h in range(HALVES):
+            nc.vector.tensor_scalar(
+                out=shift[:, h : h + 1],
+                in0=minus_mean_g[:, h : h + 1],
+                scalar1=one_over_std[:, h : h + 1],
+                scalar2=gb_cols[:, HALVES + h : HALVES + h + 1],
+                op0=ALU.mult,
+                op1=ALU.add,
+            )
 
         def apply_from_bank(engine, bank, h, pieces=1):
             z = z_pool.tile([P, GROUP], F32, name="z")

@@ -67,7 +67,7 @@ def tile_iag_pb_t_kernel(tc, T1, T2, Wf_words, Wf_scales, bn_g, bn_b, out):
             r = g // 2
             places = slice((g % 2) * TILES, (g % 2 + 1) * TILES)
             if g % 2 == 0:
-                x_pair = x_pool.tile([P, 2 * TILES, K], BF16, name="x_pair")
+                x_pair = x_pool.tile([P, 2 * TILES, K], BF16, align_bytes=256, name="x_pair")
                 pair_tiles[r] = x_pair
             if r < PAIRS_BY_GROUP:
                 load_places(r, places)
@@ -117,7 +117,7 @@ def tile_iag_pb_t_kernel(tc, T1, T2, Wf_words, Wf_scales, bn_g, bn_b, out):
         def flip_group(g):
             words = x_tiles[g].rearrange("m j c -> m (j c)").bitcast(F32)
             row_words = K // 2
-            grouped = grouped_pool.tile([P, 4 * GROUP], BF16, align_bytes=64, name="grouped")
+            grouped = grouped_pool.tile([P, 4 * GROUP], BF16, align_bytes=256, name="grouped")
             grouped_words = grouped[:].bitcast(F32).rearrange("p (r u) -> p r u", u=2)
             for b in range(GROUP_BANKS):
                 xt = banks.tile([P, 2, BANK_TILES * P], F32, tag="bank", name="xt")
@@ -225,7 +225,7 @@ def tile_iag_pb_t_kernel(tc, T1, T2, Wf_words, Wf_scales, bn_g, bn_b, out):
             )
 
         def apply_from_bank(engine, bank, h, pieces=1):
-            z = z_pool.tile([P, GROUP], F32, name="z")
+            z = z_pool.tile([P, GROUP], F32, align_bytes=256, name="z")
             for piece in range(pieces):
                 cols = slice(piece * GROUP // pieces, (piece + 1) * GROUP // pieces)
                 if engine == "scalar":
@@ -276,7 +276,7 @@ def tile_iag_pb_t_kernel(tc, T1, T2, Wf_words, Wf_scales, bn_g, bn_b, out):
             return pair_rows[:, (g % 2) * TILES : (g % 2 + 1) * TILES, :]
 
         def unflip_and_store_group(g, halves, scalar_banks):
-            o_sb = o_pool.tile([P, TILES, EMB], F32, name="o_sb")
+            o_sb = o_pool.tile([P, TILES, EMB], F32, align_bytes=256, name="o_sb")
             for b in range(GROUP_BANKS):
                 ot = banks.tile([P, BANK_TILES, EMB], F32, tag="bank", name="ot")
                 for i in range(BANK_TILES):

@@ -77,9 +77,9 @@ def tile_iag_pb_t_kernel(tc, T1, T2, Wf_words, Wf_scales, bn_g, bn_b, out):
 
         x_tiles = [load_group(0)]
 
-        w_words = consts.tile([P, EMB], U32, align_bytes=64)
+        w_words = consts.tile([P, EMB], U32, align_bytes=256)
         nc.sync.dma_start(out=w_words[:].bitcast(I32), in_=Wf_words[0].rearrange("p n t -> p (n t)").bitcast(I32))
-        w_plane = consts.tile([P, EMB], U8, align_bytes=64)
+        w_plane = consts.tile([P, EMB], U8, align_bytes=256)
         nc.vector.memset(w_plane[:].bitcast(I32), 0)
         for quadrant in range(4):
             nc.sync.dma_start(
@@ -96,7 +96,7 @@ def tile_iag_pb_t_kernel(tc, T1, T2, Wf_words, Wf_scales, bn_g, bn_b, out):
         gb_f32 = consts.tile([P, P], F32)
         nc.vector.tensor_copy(out=gb_f32[:], in_=gb_rows[:])
 
-        ident = consts.tile([P, P], F32)
+        ident = consts.tile([P, P], F32, align_bytes=256)
         make_identity(nc, ident[:])
 
         eps = consts.tile([P, 1], F32)
@@ -104,15 +104,15 @@ def tile_iag_pb_t_kernel(tc, T1, T2, Wf_words, Wf_scales, bn_g, bn_b, out):
         root_of_eps = consts.tile([P, 1], F32)
         nc.scalar.activation(out=root_of_eps[:], in_=eps[:], func=ACT.Sqrt)
 
-        x_words = consts.tile([P, GROUPS, GROUP], U32, align_bytes=64)
-        x_planes = consts.tile([P, GROUPS, GROUP], U8, align_bytes=64)
+        x_words = consts.tile([P, GROUPS, GROUP], U32, align_bytes=256)
+        x_planes = consts.tile([P, GROUPS, GROUP], U8, align_bytes=256)
         stats = consts.tile([P, HALVES, 2 * GROUPS, 3], F32)
         nc.vector.memset(stats[:, KEPT, 0 : len(S_MEASURED), 0:1], float(GROUP))
         used = {KEPT: len(S_MEASURED), AGAIN: 0}
         sums = consts.tile([P, len(S_MEASURED)], F32)
-        squares = consts.tile([P, GROUP], F32)
-        y_kept = consts.tile([P, GROUPS, GROUP], F32)
-        y_more = consts.tile([P, len(BOTH_KEPT), GROUP], F32)
+        squares = consts.tile([P, GROUP], F32, align_bytes=256)
+        y_kept = consts.tile([P, GROUPS, GROUP], F32, align_bytes=256)
+        y_more = consts.tile([P, len(BOTH_KEPT), GROUP], F32, align_bytes=256)
 
         def flip_group(g):
             words = x_tiles[g].rearrange("m j c -> m (j c)").bitcast(F32)

@@ -79,6 +79,7 @@ def tile_iag_pb_t_kernel(tc, T1, T2, Wf_words, Wf_scales, bn_g, bn_b, out):
 
         w_words = consts.tile([P, EMB], U32, align_bytes=256)
         nc.sync.dma_start(out=w_words[:].bitcast(I32), in_=Wf_words[0].rearrange("p n t -> p (n t)").bitcast(I32))
+        x_tiles.append(load_group(1))
         w_plane = consts.tile([P, EMB], U8, align_bytes=256)
         nc.vector.memset(w_plane[:].bitcast(I32), 0)
         for quadrant in range(4):
@@ -86,18 +87,19 @@ def tile_iag_pb_t_kernel(tc, T1, T2, Wf_words, Wf_scales, bn_g, bn_b, out):
                 out=w_plane[32 * quadrant : 32 * quadrant + 4, :].bitcast(I32),
                 in_=Wf_scales[0, 4 * quadrant : 4 * quadrant + 4, :].bitcast(I32),
             )
-        for g in range(1, GROUPS):
+            if quadrant % 2 == 1:
+                x_tiles.append(load_group(2 + quadrant // 2))
+        for g in range(4, GROUPS):
             x_tiles.append(load_group(g))
 
         gb_rows = consts.tile([P, P], BF16)
         nc.vector.memset(gb_rows[:], 0.0)
-        nc.scalar.dma_start(out=gb_rows[0:HALVES, :], in_=bn_g.rearrange("(h c) -> h c", h=HALVES))
-        nc.scalar.dma_start(out=gb_rows[HALVES : 2 * HALVES, :], in_=bn_b.rearrange("(h c) -> h c", h=HALVES))
         gb_f32 = consts.tile([P, P], F32)
-        nc.vector.tensor_copy(out=gb_f32[:], in_=gb_rows[:])
 
         ident = consts.tile([P, P], F32, align_bytes=256)
         make_identity(nc, ident[:])
+        nc.gpsimd.dma_start(out=gb_rows[0:HALVES, :], in_=bn_g.rearrange("(h c) -> h c", h=HALVES))
+        nc.gpsimd.dma_start(out=gb_rows[HALVES : 2 * HALVES, :], in_=bn_b.rearrange("(h c) -> h c", h=HALVES))
 
         eps = consts.tile([P, 1], F32)
         nc.vector.memset(eps[:], BN_EPS)
@@ -178,24 +180,28 @@ def tile_iag_pb_t_kernel(tc, T1, T2, Wf_words, Wf_scales, bn_g, bn_b, out):
         part_one_runs = [[0], [1]] + [[g, g + 1] for g in range(2, GROUPS, RUN)]
         y_tiles = {}
         gb_cols = consts.tile([P, 2 * HALVES], F32)
+        GB_STEP = 4
         lag = 2
         for r in range(len(part_one_runs) + lag):
             grouped_tiles = {}
             if r < len(part_one_runs):
                 for g in part_one_runs[r]:
                     grouped_tiles[g] = flip_group(g)
-            if r == 0:
+            if r == GB_STEP:
                 gb_bank = banks.tile([P, 2, BANK_TILES * P], F32, tag="bank", name="gb_bank")
                 nc.tensor.transpose(gb_bank[:, 0, 0:P], gb_f32[:], ident[:])
                 nc.vector.tensor_copy(out=gb_cols[:], in_=gb_bank[:, 0, 0 : 2 * HALVES])
             if r >= lag:
                 for g in part_one_runs[r - lag]:
                     y_tiles[g] = [multiply(g, h) for h in range(HALVES)]
+            if r >= lag:
                 for g in part_one_runs[r - lag]:
                     measure_group(g, y_tiles[g])
             if r < len(part_one_runs):
                 for g in part_one_runs[r]:
                     quantise_group(g, grouped_tiles[g])
+            if r == GB_STEP - 1:
+                nc.vector.tensor_copy(out=gb_f32[:], in_=gb_rows[:])
 
         order = [FIRST, FIRST + 1] + list(range(FIRST))
         for g in order[2:6]:

@@ -32,7 +32,7 @@ RUNS = GROUPS // RUN
 AHEAD = 8
 BOTH_KEPT = (GROUPS - 4, GROUPS - 3)
 S_MEASURED = BOTH_KEPT
-PAIRS_BY_GROUP = 2
+PAIRS_BY_GROUP = 3
 FIRST = GROUPS - 2
 
 FLOPS = 2 * ROWS * K * EMB
@@ -180,8 +180,11 @@ def tile_iag_pb_t_kernel(tc, T1, T2, Wf_words, Wf_scales, bn_g, bn_b, out):
         part_one_runs = [[0], [1]] + [[g, g + 1] for g in range(2, GROUPS, RUN)]
         y_tiles = {}
         gb_cols = consts.tile([P, 2 * HALVES], F32)
-        GB_STEP = 4
+        GB_STEP = 6
         lag = 2
+        multiplied_in = [[], [], [0, 1]] + [
+            [g for g in (2 * r - 5, 2 * r - 4) if 2 <= g < GROUPS] for r in range(3, len(part_one_runs) + lag)
+        ]
         for r in range(len(part_one_runs) + lag):
             grouped_tiles = {}
             if r < len(part_one_runs):
@@ -191,16 +194,14 @@ def tile_iag_pb_t_kernel(tc, T1, T2, Wf_words, Wf_scales, bn_g, bn_b, out):
                 gb_bank = banks.tile([P, 2, BANK_TILES * P], F32, tag="bank", name="gb_bank")
                 nc.tensor.transpose(gb_bank[:, 0, 0:P], gb_f32[:], ident[:])
                 nc.vector.tensor_copy(out=gb_cols[:], in_=gb_bank[:, 0, 0 : 2 * HALVES])
-            if r >= lag:
-                for g in part_one_runs[r - lag]:
-                    y_tiles[g] = [multiply(g, h) for h in range(HALVES)]
-            if r >= lag:
-                for g in part_one_runs[r - lag]:
-                    measure_group(g, y_tiles[g])
+            for g in multiplied_in[r]:
+                y_tiles[g] = [multiply(g, h) for h in range(HALVES)]
+            for g in multiplied_in[r]:
+                measure_group(g, y_tiles[g])
             if r < len(part_one_runs):
                 for g in part_one_runs[r]:
                     quantise_group(g, grouped_tiles[g])
-            if r == GB_STEP - 1:
+            if r == GB_STEP - 3:
                 nc.vector.tensor_copy(out=gb_f32[:], in_=gb_rows[:])
 
         order = [FIRST, FIRST + 1] + list(range(FIRST))

from contextlib import ExitStack

import concourse.mybir as mybir
from concourse.masks import make_identity

F32 = mybir.dt.float32
BF16 = mybir.dt.bfloat16
I32 = mybir.dt.int32
U32 = mybir.dt.uint32
U8 = mybir.dt.uint8
FP8X4 = mybir.dt.float8_e4m3fn_x4
ACT = mybir.ActivationFunctionType
ALU = mybir.AluOpType

P = 128
ROWS = 4 * 2048
STREAM = 256
K = 2 * STREAM
EMB = 256
HALVES = EMB // P
KEPT = 0
AGAIN = 1
BN_EPS = 1e-5

GROUP = 512
TILES = GROUP // P
GROUPS = ROWS // GROUP
BANK_TILES = 2
GROUP_BANKS = TILES // BANK_TILES
RUN = 2
RUNS = GROUPS // RUN
AHEAD = 8
BOTH_KEPT = (GROUPS - 4, GROUPS - 3)
S_MEASURED = BOTH_KEPT
PAIRS_BY_GROUP = 3
FIRST = GROUPS - 2

FLOPS = 2 * ROWS * K * EMB


def tile_iag_pb_t_kernel(tc, T1, T2, Wf_words, Wf_scales, bn_g, bn_b, out):
    nc = tc.nc
    streams = (T1.flatten_outer_dims(), T2.flatten_outer_dims())
    out_rows = out.flatten_outer_dims()

    with ExitStack() as ctx:
        consts = ctx.enter_context(tc.tile_pool(name="consts", bufs=1))
        x_pool = ctx.enter_context(tc.tile_pool(name="x", bufs=GROUPS // 2))
        grouped_pool = ctx.enter_context(tc.tile_pool(name="grouped", bufs=AHEAD))
        z_pool = ctx.enter_context(tc.tile_pool(name="z", bufs=AHEAD))
        o_pool = ctx.enter_context(tc.tile_pool(name="o", bufs=AHEAD))
        banks = ctx.enter_context(tc.psum_pool(name="banks", bufs=8))
        ctx.enter_context(tc.manual_schedule())

        pair_tiles = {}

        def load_places(r, places):
            for s in range(2):
                nc.sync.dma_start(
                    out=pair_tiles[r][:, places, s * STREAM : (s + 1) * STREAM],
                    in_=streams[s][r * 2 * GROUP : (r + 1) * 2 * GROUP, :].rearrange("(m j) c -> m j c", j=2 * TILES)[
                        :, places, :
                    ],
                )

        def load_group(g):
            r = g // 2
            places = slice((g % 2) * TILES, (g % 2 + 1) * TILES)
            if g % 2 == 0:
                x_pair = x_pool.tile([P, 2 * TILES, K], BF16, align_bytes=256, name="x_pair")
                pair_tiles[r] = x_pair
            if r < PAIRS_BY_GROUP:
                load_places(r, places)
            elif g % 2 == 0:
                load_places(r, slice(0, 2 * TILES))
            return pair_tiles[r][:, places, :]

        x_tiles = [load_group(0)]

        w_words = consts.tile([P, EMB], U32, align_bytes=256)
        nc.sync.dma_start(out=w_words[:].bitcast(I32), in_=Wf_words[0].rearrange("p n t -> p (n t)").bitcast(I32))
        x_tiles.append(load_group(1))
        w_plane = consts.tile([P, EMB], U8, align_bytes=256)
        nc.vector.memset(w_plane[:].bitcast(I32), 0)
        for quadrant in range(4):
            nc.sync.dma_start(
                out=w_plane[32 * quadrant : 32 * quadrant + 4, :].bitcast(I32),
                in_=Wf_scales[0, 4 * quadrant : 4 * quadrant + 4, :].bitcast(I32),
            )
            if quadrant % 2 == 1:
                x_tiles.append(load_group(2 + quadrant // 2))
        for g in range(4, GROUPS):
            x_tiles.append(load_group(g))

        gb_rows = consts.tile([P, P], BF16)
        nc.vector.memset(gb_rows[:], 0.0)
        gb_f32 = consts.tile([P, P], F32)

        ident = consts.tile([P, P], F32, align_bytes=256)
        make_identity(nc, ident[:])
        nc.gpsimd.dma_start(out=gb_rows[0:HALVES, :], in_=bn_g.rearrange("(h c) -> h c", h=HALVES))
        nc.gpsimd.dma_start(out=gb_rows[HALVES : 2 * HALVES, :], in_=bn_b.rearrange("(h c) -> h c", h=HALVES))

        eps = consts.tile([P, 1], F32)
        nc.vector.memset(eps[:], BN_EPS)
        root_of_eps = consts.tile([P, 1], F32)
        nc.scalar.activation(out=root_of_eps[:], in_=eps[:], func=ACT.Sqrt)

        x_words = consts.tile([P, GROUPS, GROUP], U32, align_bytes=256)
        x_planes = consts.tile([P, GROUPS, GROUP], U8, align_bytes=256)
        stats = consts.tile([P, HALVES, 2 * GROUPS, 3], F32)
        nc.vector.memset(stats[:, KEPT, 0 : len(S_MEASURED), 0:1], float(GROUP))
        used = {KEPT: len(S_MEASURED), AGAIN: 0}
        sums = consts.tile([P, len(S_MEASURED)], F32)
        squares = consts.tile([P, GROUP], F32, align_bytes=256)
        y_kept = consts.tile([P, GROUPS, GROUP], F32, align_bytes=256)
        y_more = consts.tile([P, len(BOTH_KEPT), GROUP], F32, align_bytes=256)

        def flip_group(g):
            words = x_tiles[g].rearrange("m j c -> m (j c)").bitcast(F32)
            row_words = K // 2
            grouped = grouped_pool.tile([P, 4 * GROUP], BF16, align_bytes=256, name="grouped")
            grouped_words = grouped[:].bitcast(F32).rearrange("p (r u) -> p r u", u=2)
            for b in range(GROUP_BANKS):
                xt = banks.tile([P, 2, BANK_TILES * P], F32, tag="bank", name="xt")
                for i in range(BANK_TILES):
                    j = b * BANK_TILES + i
                    for u in range(2):
                        nc.tensor.transpose(
                            xt[:, u, i * P : (i + 1) * P],
                            words[:, j * row_words + u : (j + 1) * row_words : 2],
                            ident[:],
                        )
                bank_rows = slice(b * BANK_TILES * P, (b + 1) * BANK_TILES * P)
                nc.scalar.copy(out=grouped_words[:, bank_rows, :], in_=xt[:].rearrange("p u r -> p r u"))
            return grouped

        def quantise_group(g, grouped):
            nc.vector.quantize_mx(out=x_words[:, g, :].bitcast(FP8X4), scales=x_planes[:, g, :], in_=grouped[:])

        def multiply(g, h):
            y = banks.tile([P, GROUP], F32, tag="bank", name="y")
            nc.tensor.matmul_mx(
                out=y[:],
                lhsT=w_words[:, h * P : (h + 1) * P].bitcast(FP8X4),
                lhsT_scale=w_plane[:, h * P : (h + 1) * P],
                rhs=x_words[:, g, :].bitcast(FP8X4),
                rhs_scale=x_planes[:, g, :],
                start=True,
                stop=True,
            )
            return y

        def measure_group(g, products):
            for h in range(HALVES):
                if h == AGAIN or g not in S_MEASURED:
                    nc.vector.bn_stats(
                        out=stats[:, h, used[h] : used[h] + 2, :].rearrange("p t s -> p (t s)"), in_=products[h][:]
                    )
                    used[h] = used[h] + 2
            if g in S_MEASURED:
                i = S_MEASURED.index(g)
                nc.scalar.activation(
                    out=y_kept[:, g, :], in_=products[KEPT][:], func=ACT.Identity, accum_out=sums[:, i : i + 1]
                )
                nc.scalar.mul(out=stats[:, KEPT, i, 1:2], in_=sums[:, i : i + 1], mul=1.0 / GROUP)
                nc.scalar.activation(
                    out=squares[:],
                    in_=products[KEPT][:],
                    func=ACT.Square,
                    scale=-1.0,
                    bias=stats[:, KEPT, i, 1:2],
                    accum_out=stats[:, KEPT, i, 2:3],
                )
            elif g != FIRST:
                nc.scalar.copy(out=y_kept[:, g, :], in_=products[KEPT][:])
            if g in BOTH_KEPT:
                nc.scalar.copy(out=y_more[:, BOTH_KEPT.index(g), :], in_=products[AGAIN][:])

        part_one_runs = [[0], [1]] + [[g, g + 1] for g in range(2, GROUPS, RUN)]
        y_tiles = {}
        gb_cols = consts.tile([P, 2 * HALVES], F32)
        GB_STEP = 6
        lag = 2
        multiplied_in = [[], [], [0, 1]] + [
            [g for g in (2 * r - 5, 2 * r - 4) if 2 <= g < GROUPS] for r in range(3, len(part_one_runs) + lag)
        ]
        for r in range(len(part_one_runs) + lag):
            grouped_tiles = {}
            if r < len(part_one_runs):
                for g in part_one_runs[r]:
                    grouped_tiles[g] = flip_group(g)
            if r == GB_STEP:
                gb_bank = banks.tile([P, 2, BANK_TILES * P], F32, tag="bank", name="gb_bank")
                nc.tensor.transpose(gb_bank[:, 0, 0:P], gb_f32[:], ident[:])
                nc.vector.tensor_copy(out=gb_cols[:], in_=gb_bank[:, 0, 0 : 2 * HALVES])
            for g in multiplied_in[r]:
                y_tiles[g] = [multiply(g, h) for h in range(HALVES)]
            for g in multiplied_in[r]:
                measure_group(g, y_tiles[g])
            if r < len(part_one_runs):
                for g in part_one_runs[r]:
                    quantise_group(g, grouped_tiles[g])
            if r == GB_STEP - 3:
                nc.vector.tensor_copy(out=gb_f32[:], in_=gb_rows[:])

        order = [FIRST, FIRST + 1] + list(range(FIRST))
        for g in order[2:6]:
            y_tiles[g][AGAIN] = multiply(g, AGAIN)

        mean_var = consts.tile([P, HALVES, 2], F32)
        for h in range(HALVES):
            nc.vector.bn_aggr(out=mean_var[:, h, :], in_=stats[:, h, 0 : used[h], :].rearrange("p t s -> p (t s)"))
        std = consts.tile([P, HALVES], F32)
        nc.scalar.activation(out=std[:], in_=mean_var[:, :, 1], func=ACT.Sqrt, bias=eps[:])
        minus_mean_g = consts.tile([P, HALVES], F32)
        nc.vector.tensor_mul(out=minus_mean_g[:], in0=mean_var[:, :, 0], in1=gb_cols[:, 0:HALVES])
        nc.vector.tensor_scalar_mul(out=minus_mean_g[:], in0=minus_mean_g[:], scalar1=-1.0)
        one_over_std = consts.tile([P, HALVES], F32)
        nc.vector.reciprocal(out=one_over_std[:], in_=std[:])
        gain = consts.tile([P, HALVES], F32)
        shift = consts.tile([P, HALVES], F32)
        nc.vector.tensor_mul(out=gain[:], in0=one_over_std[:], in1=gb_cols[:, 0:HALVES])
        for h in range(HALVES):
            nc.vector.tensor_scalar(
                out=shift[:, h : h + 1],
                in0=minus_mean_g[:, h : h + 1],
                scalar1=one_over_std[:, h : h + 1],
                scalar2=gb_cols[:, HALVES + h : HALVES + h + 1],
                op0=ALU.mult,
                op1=ALU.add,
            )

        def apply_from_bank(engine, bank, h, pieces=1):
            z = z_pool.tile([P, GROUP], F32, align_bytes=256, name="z")
            for piece in range(pieces):
                cols = slice(piece * GROUP // pieces, (piece + 1) * GROUP // pieces)
                if engine == "scalar":
                    nc.scalar.activation(
                        out=z[:, cols],
                        in_=bank[:, cols],
                        func=ACT.Identity,
                        bias=shift[:, h : h + 1],
                        scale=gain[:, h : h + 1],
                    )
                else:
                    nc.vector.tensor_scalar(
                        out=z[:, cols],
                        in0=bank[:, cols],
                        scalar1=gain[:, h : h + 1],
                        scalar2=shift[:, h : h + 1],
                        op0=ALU.mult,
                        op1=ALU.add,
                    )
            return z[:]

        def apply_in_place(y):
            nc.gpsimd.tensor_scalar(
                out=y[0], in0=y[0], scalar1=gain[:, y[1] : y[1] + 1], scalar2=shift[:, y[1] : y[1] + 1], op0=ALU.mult, op1=ALU.add
            )
            return y[0]

        def apply_group(g, engine):
            if g == FIRST:
                return {
                    KEPT: apply_from_bank("scalar", y_tiles[g][KEPT], KEPT, pieces=GROUP_BANKS),
                    AGAIN: apply_from_bank("vector", y_tiles[g][AGAIN], AGAIN, pieces=GROUP_BANKS),
                }
            if g in BOTH_KEPT:
                return {
                    KEPT: apply_in_place((y_kept[:, g, :], KEPT)),
                    AGAIN: apply_in_place((y_more[:, BOTH_KEPT.index(g), :], AGAIN)),
                }
            return {
                KEPT: apply_in_place((y_kept[:, g, :], KEPT)),
                AGAIN: apply_from_bank(engine, y_tiles[g][AGAIN], AGAIN),
            }

        def group_rows(g):
            pair_rows = out_rows[(g // 2) * 2 * GROUP : (g // 2 + 1) * 2 * GROUP, :].rearrange(
                "(m j) n -> m j n", j=2 * TILES
            )
            return pair_rows[:, (g % 2) * TILES : (g % 2 + 1) * TILES, :]

        def unflip_and_store_group(g, halves, scalar_banks):
            o_sb = o_pool.tile([P, TILES, EMB], F32, align_bytes=256, name="o_sb")
            for b in range(GROUP_BANKS):
                ot = banks.tile([P, BANK_TILES, EMB], F32, tag="bank", name="ot")
                for i in range(BANK_TILES):
                    j = b * BANK_TILES + i
                    for h in range(HALVES):
                        nc.tensor.transpose(ot[:, i, h * P : (h + 1) * P], halves[h][:, j * P : (j + 1) * P], ident[:])
                o_rows = o_sb[:, b * BANK_TILES : (b + 1) * BANK_TILES, :]
                if b in scalar_banks:
                    nc.scalar.activation(out=o_rows, in_=ot[:], func=ACT.Relu)
                else:
                    nc.vector.tensor_scalar_max(out=o_rows, in0=ot[:], scalar1=0.0)
                if g == FIRST:
                    nc.sync.dma_start(
                        out=group_rows(g)[
                            :, b * BANK_TILES : (b + 1) * BANK_TILES, :
                        ],
                        in_=o_rows,
                    )
            if g != FIRST:
                nc.sync.dma_start(
                    out=group_rows(g), in_=o_sb[:]
                )

        ahead = 3
        engines = ("vector", "scalar")
        applied = {}
        for n in range(ahead):
            applied[order[n]] = apply_group(order[n], engines[n % 2])
        for n in range(GROUPS):
            unflip_and_store_group(order[n], applied[order[n]], (1,))
            if n % 2 == 1 and n >= 3:
                for g in order[n + ahead : n + ahead + 2]:
                    if g not in BOTH_KEPT:
                        y_tiles[g][AGAIN] = multiply(g, AGAIN)
            if n + ahead < GROUPS:
                applied[order[n + ahead]] = apply_group(order[n + ahead], engines[(n + ahead) % 2])
